import numpy as np
import ml_dtypes

BF16 = ml_dtypes.bfloat16


def bf(x):
    return np.asarray(x, np.float32).astype(BF16)


def f32(x):
    return np.asarray(x, np.float32)


def f64(x):
    return np.asarray(x).astype(np.float64)


def striped(idx):
    return np.tile(idx.reshape(-1, 16).T, (8, 1))


C, S, K, N = 128, 512, 4, 2048


def setup_inputs():
    return {"x": f32(np.random.standard_normal((C, S))), "offs": striped(np.concatenate([np.random.permutation(S) for _ in range(K)]))}


def reference(x, offs):
    idx = offs[:16].T.reshape(-1)
    return f64(x)[:, idx].reshape(C, K, S).sum(axis=1)

@@ -1,0 +1,34 @@
+import concourse.mybir as mybir
+
+F32 = mybir.dt.float32
+U16 = mybir.dt.uint16
+ADD = mybir.AluOpType.add
+
+SAMPLES = 128
+NODES = 512
+LEAVES = 512
+LEVELS = 4
+PER_COLUMN = 16
+
+
+def tile_roottoleafsums_kernel(tc, x, offs, out):
+    nc = tc.nc
+    level_columns = LEAVES // PER_COLUMN
+    with tc.tile_pool(name="held", bufs=1) as held:
+        offsets = held.tile([SAMPLES, LEVELS * level_columns], U16, name="offsets")
+        nodes = held.tile([SAMPLES, NODES], F32, name="nodes")
+
+        nc.sync.dma_start(offsets[:], offs)
+        nc.scalar.dma_start(nodes[:], x)
+
+        sums = [held.tile([SAMPLES, LEAVES], F32, name=f"sum{level}") for level in range(LEVELS)]
+        for level in range(LEVELS):
+            picked = nodes[:].indirect(
+                offsets[:, level * level_columns : (level + 1) * level_columns]
+            )
+            if level == 0:
+                nc.vector.tensor_copy(sums[0][:], picked)
+            else:
+                nc.vector.tensor_tensor(sums[level][:], picked, sums[level - 1][:], ADD)
+
+        nc.sync.dma_start(out, sums[LEVELS - 1][:])

@@ -9,26 +9,31 @@ NODES = 512
 LEAVES = 512
 LEVELS = 4
 PER_COLUMN = 16
+HALVES = 2
+HALF = LEAVES // HALVES
 
 
 def tile_roottoleafsums_kernel(tc, x, offs, out):
     nc = tc.nc
-    level_columns = LEAVES // PER_COLUMN
     with tc.tile_pool(name="held", bufs=1) as held:
-        offsets = held.tile([SAMPLES, LEVELS * level_columns], U16, name="offsets")
+        offsets = held.tile([SAMPLES, LEVELS * LEAVES // PER_COLUMN], U16, name="offsets")
         nodes = held.tile([SAMPLES, NODES], F32, name="nodes")
 
         nc.sync.dma_start(offsets[:], offs)
         nc.scalar.dma_start(nodes[:], x)
 
-        sums = [held.tile([SAMPLES, LEAVES], F32, name=f"sum{level}") for level in range(LEVELS)]
+        store_queues = [nc.sync, nc.scalar]
+        before = [None] * HALVES
         for level in range(LEVELS):
-            picked = nodes[:].indirect(
-                offsets[:, level * level_columns : (level + 1) * level_columns]
-            )
-            if level == 0:
-                nc.vector.tensor_copy(sums[0][:], picked)
-            else:
-                nc.vector.tensor_tensor(sums[level][:], picked, sums[level - 1][:], ADD)
+            for half in range(HALVES):
+                first = (level * LEAVES + half * HALF) // PER_COLUMN
+                picked = nodes[:].indirect(offsets[:, first : first + HALF // PER_COLUMN])
+                total = held.tile([SAMPLES, HALF], F32, name=f"total{level}_{half}")
+                if level == 0:
+                    nc.vector.tensor_copy(total[:], picked)
+                else:
+                    nc.vector.tensor_tensor(total[:], picked, before[half][:], ADD)
+                before[half] = total
 
-        nc.sync.dma_start(out, sums[LEVELS - 1][:])
+        for half in range(HALVES):
+            store_queues[half].dma_start(out[:, half * HALF : (half + 1) * HALF], before[half][:])

@@ -22,7 +22,6 @@ def tile_roottoleafsums_kernel(tc, x, offs, out):
         nc.sync.dma_start(offsets[:], offs)
         nc.scalar.dma_start(nodes[:], x)
 
-        store_queues = [nc.sync, nc.scalar]
         before = [None] * HALVES
         for level in range(LEVELS):
             for half in range(HALVES):
@@ -36,4 +35,4 @@ def tile_roottoleafsums_kernel(tc, x, offs, out):
                 before[half] = total
 
         for half in range(HALVES):
-            store_queues[half].dma_start(out[:, half * HALF : (half + 1) * HALF], before[half][:])
+            nc.sync.dma_start(out[:, half * HALF : (half + 1) * HALF], before[half][:])

@@ -11,6 +11,7 @@ LEVELS = 4
 PER_COLUMN = 16
 HALVES = 2
 HALF = LEAVES // HALVES
+QUARTER = HALF // 2
 
 
 def tile_roottoleafsums_kernel(tc, x, offs, out):
@@ -23,7 +24,7 @@ def tile_roottoleafsums_kernel(tc, x, offs, out):
         nc.scalar.dma_start(nodes[:], x)
 
         before = [None] * HALVES
-        for level in range(LEVELS):
+        for level in range(LEVELS - 1):
             for half in range(HALVES):
                 first = (level * LEAVES + half * HALF) // PER_COLUMN
                 picked = nodes[:].indirect(offsets[:, first : first + HALF // PER_COLUMN])
@@ -34,5 +35,15 @@ def tile_roottoleafsums_kernel(tc, x, offs, out):
                     nc.vector.tensor_tensor(total[:], picked, before[half][:], ADD)
                 before[half] = total
 
-        for half in range(HALVES):
-            nc.sync.dma_start(out[:, half * HALF : (half + 1) * HALF], before[half][:])
+        store_queues = [nc.sync, nc.scalar]
+        for quarter in range(LEAVES // QUARTER):
+            half, side = divmod(quarter, HALF // QUARTER)
+            first = ((LEVELS - 1) * LEAVES + quarter * QUARTER) // PER_COLUMN
+            picked = nodes[:].indirect(offsets[:, first : first + QUARTER // PER_COLUMN])
+            total = held.tile([SAMPLES, QUARTER], F32, name=f"total_last_{quarter}")
+            nc.vector.tensor_tensor(
+                total[:], picked, before[half][:, side * QUARTER : (side + 1) * QUARTER], ADD
+            )
+            store_queues[quarter % 2].dma_start(
+                out[:, quarter * QUARTER : (quarter + 1) * QUARTER], total[:]
+            )

@@ -11,7 +11,6 @@ LEVELS = 4
 PER_COLUMN = 16
 HALVES = 2
 HALF = LEAVES // HALVES
-QUARTER = HALF // 2
 
 
 def tile_roottoleafsums_kernel(tc, x, offs, out):
@@ -23,27 +22,17 @@ def tile_roottoleafsums_kernel(tc, x, offs, out):
         nc.sync.dma_start(offsets[:], offs)
         nc.scalar.dma_start(nodes[:], x)
 
-        before = [None] * HALVES
-        for level in range(LEVELS - 1):
+        totals = [held.tile([SAMPLES, LEAVES], F32, name=f"total{level}") for level in range(LEVELS)]
+        for level in range(LEVELS):
             for half in range(HALVES):
+                leaves = slice(half * HALF, (half + 1) * HALF)
                 first = (level * LEAVES + half * HALF) // PER_COLUMN
                 picked = nodes[:].indirect(offsets[:, first : first + HALF // PER_COLUMN])
-                total = held.tile([SAMPLES, HALF], F32, name=f"total{level}_{half}")
                 if level == 0:
-                    nc.vector.tensor_copy(total[:], picked)
+                    nc.vector.tensor_copy(totals[0][:, leaves], picked)
                 else:
-                    nc.vector.tensor_tensor(total[:], picked, before[half][:], ADD)
-                before[half] = total
+                    nc.vector.tensor_tensor(
+                        totals[level][:, leaves], picked, totals[level - 1][:, leaves], ADD
+                    )
 
-        store_queues = [nc.sync, nc.scalar]
-        for quarter in range(LEAVES // QUARTER):
-            half, side = divmod(quarter, HALF // QUARTER)
-            first = ((LEVELS - 1) * LEAVES + quarter * QUARTER) // PER_COLUMN
-            picked = nodes[:].indirect(offsets[:, first : first + QUARTER // PER_COLUMN])
-            total = held.tile([SAMPLES, QUARTER], F32, name=f"total_last_{quarter}")
-            nc.vector.tensor_tensor(
-                total[:], picked, before[half][:, side * QUARTER : (side + 1) * QUARTER], ADD
-            )
-            store_queues[quarter % 2].dma_start(
-                out[:, quarter * QUARTER : (quarter + 1) * QUARTER], total[:]
-            )
+        nc.sync.dma_start(out, totals[LEVELS - 1][:])

@@ -20,19 +20,25 @@ def tile_roottoleafsums_kernel(tc, x, offs, out):
         nodes = held.tile([SAMPLES, NODES], F32, name="nodes")
 
         nc.sync.dma_start(offsets[:], offs)
-        nc.scalar.dma_start(nodes[:], x)
+        load_queues = [nc.scalar, nc.sync]
+        block = NODES // 4
+        for b in range(4):
+            load_queues[b % 2].dma_start(
+                nodes[:, b * block : (b + 1) * block], x[:, b * block : (b + 1) * block]
+            )
 
-        totals = [held.tile([SAMPLES, LEAVES], F32, name=f"total{level}") for level in range(LEVELS)]
+        store_queues = [nc.sync, nc.scalar]
+        before = [None] * HALVES
         for level in range(LEVELS):
             for half in range(HALVES):
-                leaves = slice(half * HALF, (half + 1) * HALF)
                 first = (level * LEAVES + half * HALF) // PER_COLUMN
                 picked = nodes[:].indirect(offsets[:, first : first + HALF // PER_COLUMN])
+                total = held.tile([SAMPLES, HALF], F32, name=f"total{level}_{half}")
                 if level == 0:
-                    nc.vector.tensor_copy(totals[0][:, leaves], picked)
+                    nc.vector.tensor_copy(total[:], picked)
                 else:
-                    nc.vector.tensor_tensor(
-                        totals[level][:, leaves], picked, totals[level - 1][:, leaves], ADD
-                    )
+                    nc.vector.tensor_tensor(total[:], picked, before[half][:], ADD)
+                before[half] = total
 
-        nc.sync.dma_start(out, totals[LEVELS - 1][:])
+        for half in range(HALVES):
+            store_queues[half].dma_start(out[:, half * HALF : (half + 1) * HALF], before[half][:])

@@ -27,7 +27,6 @@ def tile_roottoleafsums_kernel(tc, x, offs, out):
                 nodes[:, b * block : (b + 1) * block], x[:, b * block : (b + 1) * block]
             )
 
-        store_queues = [nc.sync, nc.scalar]
         before = [None] * HALVES
         for level in range(LEVELS):
             for half in range(HALVES):
@@ -41,4 +40,4 @@ def tile_roottoleafsums_kernel(tc, x, offs, out):
                 before[half] = total
 
         for half in range(HALVES):
-            store_queues[half].dma_start(out[:, half * HALF : (half + 1) * HALF], before[half][:])
+            nc.scalar.dma_start(out[:, half * HALF : (half + 1) * HALF], before[half][:])

@@ -20,10 +20,9 @@ def tile_roottoleafsums_kernel(tc, x, offs, out):
         nodes = held.tile([SAMPLES, NODES], F32, name="nodes")
 
         nc.sync.dma_start(offsets[:], offs)
-        load_queues = [nc.scalar, nc.sync]
         block = NODES // 4
         for b in range(4):
-            load_queues[b % 2].dma_start(
+            nc.sync.dma_start(
                 nodes[:, b * block : (b + 1) * block], x[:, b * block : (b + 1) * block]
             )
 

@@ -20,8 +20,8 @@ def tile_roottoleafsums_kernel(tc, x, offs, out):
         nodes = held.tile([SAMPLES, NODES], F32, name="nodes")
 
         nc.sync.dma_start(offsets[:], offs)
-        block = NODES // 4
-        for b in range(4):
+        block = NODES // 2
+        for b in range(2):
             nc.sync.dma_start(
                 nodes[:, b * block : (b + 1) * block], x[:, b * block : (b + 1) * block]
             )

@@ -20,11 +20,7 @@ def tile_roottoleafsums_kernel(tc, x, offs, out):
         nodes = held.tile([SAMPLES, NODES], F32, name="nodes")
 
         nc.sync.dma_start(offsets[:], offs)
-        block = NODES // 2
-        for b in range(2):
-            nc.sync.dma_start(
-                nodes[:, b * block : (b + 1) * block], x[:, b * block : (b + 1) * block]
-            )
+        nc.sync.dma_start(nodes[:], x)
 
         before = [None] * HALVES
         for level in range(LEVELS):

@@ -19,8 +19,8 @@ def tile_roottoleafsums_kernel(tc, x, offs, out):
         offsets = held.tile([SAMPLES, LEVELS * LEAVES // PER_COLUMN], U16, name="offsets")
         nodes = held.tile([SAMPLES, NODES], F32, name="nodes")
 
-        nc.sync.dma_start(offsets[:], offs)
         nc.sync.dma_start(nodes[:], x)
+        nc.sync.dma_start(offsets[:], offs)
 
         before = [None] * HALVES
         for level in range(LEVELS):

import concourse.mybir as mybir

F32 = mybir.dt.float32
U16 = mybir.dt.uint16
ADD = mybir.AluOpType.add

SAMPLES = 128
NODES = 512
LEAVES = 512
LEVELS = 4
PER_COLUMN = 16
HALVES = 2
HALF = LEAVES // HALVES


def tile_roottoleafsums_kernel(tc, x, offs, out):
    nc = tc.nc
    with tc.tile_pool(name="held", bufs=1) as held:
        offsets = held.tile([SAMPLES, LEVELS * LEAVES // PER_COLUMN], U16, name="offsets")
        nodes = held.tile([SAMPLES, NODES], F32, name="nodes")

        nc.sync.dma_start(nodes[:], x)
        nc.sync.dma_start(offsets[:], offs)

        before = [None] * HALVES
        for level in range(LEVELS):
            for half in range(HALVES):
                first = (level * LEAVES + half * HALF) // PER_COLUMN
                picked = nodes[:].indirect(offsets[:, first : first + HALF // PER_COLUMN])
                total = held.tile([SAMPLES, HALF], F32, name=f"total{level}_{half}")
                if level == 0:
                    nc.vector.tensor_copy(total[:], picked)
                else:
                    nc.vector.tensor_tensor(total[:], picked, before[half][:], ADD)
                before[half] = total

        for half in range(HALVES):
            nc.scalar.dma_start(out[:, half * HALF : (half + 1) * HALF], before[half][:])
